import numpy as np
import ml_dtypes


def mxq(x, axis, fmt="e4m3"):
    dtype, down = {"e4m3": (ml_dtypes.float8_e4m3fn, 7), "e5m2": (ml_dtypes.float8_e5m2, 14)}[fmt]
    v = np.moveaxis(np.asarray(x, np.float32).astype(ml_dtypes.bfloat16).astype(np.float64), axis, -1)
    blocks = v.reshape(v.shape[:-1] + (-1, 32))
    amax = np.abs(blocks).max(-1, keepdims=True)
    byte = np.maximum(np.where(amax > 0, np.frexp(amax)[1] - 1 + 127, 0) - down, 1)
    scale = np.exp2(byte - 127.0)
    codes = (blocks / scale).astype(np.float32).astype(dtype).astype(np.float64)
    return np.moveaxis((codes * scale).reshape(v.shape), -1, axis)


WIDE = False


def mx_kscale(k):
    if not WIDE:
        return np.ones(k)
    levels = np.array([10, -10, 5, -5, 0])
    a = np.random.permutation(np.resize(levels, k // 512 * 4)).reshape(k // 512, 4)
    idx = np.arange(k)
    return np.exp2(a[idx // 512, idx % 128 // 32])


BF16 = ml_dtypes.bfloat16


def bf(x):
    return np.asarray(x, np.float32).astype(BF16)


def f64(x):
    return np.asarray(x).astype(np.float64)


N, C, H, W, HIDDEN, OUT = 8, 512, 8, 8, 8192, 768
P = H * W
M = N * P


def leaky_relu(v):
    return np.where(v >= 0.0, v, 0.01 * v)


def setup_inputs():
    s, t = mx_kscale(M), mx_kscale(HIDDEN)
    strong = np.where(np.random.random((M, M)) * N < 1.0, 1.0, 0.02)
    weight = np.random.random((M, M)) * strong * 2.0 / P
    hid = leaky_relu(np.random.standard_normal((M, HIDDEN)) * 0.8 - 0.4)
    return {"weight": bf(weight * s[None, :]),
            "hid": bf(hid * t[None, :] / s[:, None]),
            "W2": bf(np.random.standard_normal((OUT, HIDDEN)) * 3.0 / np.sqrt(HIDDEN) / t[None, :]),
            "b2": bf(np.random.standard_normal(OUT) * 0.2 - 0.3)}


def reference(weight, hid, W2, b2):
    agg = mxq(f64(weight), 1, "e4m3") @ mxq(f64(hid), 0, "e4m3")
    y = leaky_relu((mxq(agg, 1, "e4m3") @ mxq(f64(W2), 1, "e4m3").T) + f64(b2))
    y = y.reshape(N, H, W, -1).transpose(0, 3, 1, 2)
    return y.max(axis=0, keepdims=True)

@@ -1,0 +1,203 @@
+import concourse.mybir as mybir
+from concourse.masks import make_identity
+
+F32 = mybir.dt.float32
+BF16 = mybir.dt.bfloat16
+U32 = mybir.dt.uint32
+U8 = mybir.dt.uint8
+FP8X4 = mybir.dt.float8_e4m3fn_x4
+ALU = mybir.AluOpType
+
+P = 128
+PACK = 4
+K_PASS = P * PACK
+HALF = K_PASS // 2
+
+NODES = 512
+HIDDEN = 8192
+OUT = 768
+SAMPLES = 8
+PIXELS = 64
+SLOPE = 0.01
+
+NODE_TILES = NODES // P
+OUT_TILES = OUT // P
+PASSES = HIDDEN // K_PASS
+CHUNK_PASSES = 2
+CHUNK = CHUNK_PASSES * K_PASS
+CHUNKS = HIDDEN // CHUNK
+FIRST_GROUP = 4
+
+FLOPS = 2 * NODES * NODES * HIDDEN + 2 * NODES * HIDDEN * OUT
+
+
+def flip_two_row_tiles(nc, banks, identity, words, tile0, word0, grouped_words):
+    bank = banks.tile([P, PACK, P], F32, tag="bank")
+    for a in range(2):
+        for u in range(2):
+            nc.tensor.transpose(
+                bank[:, 2 * a + u, :],
+                words[:, tile0 + a, word0 + u * P : word0 + (u + 1) * P],
+                identity[:],
+            )
+    nc.scalar.copy(
+        out=grouped_words[:, tile0 * P : (tile0 + 2) * P, :].rearrange("p (a r) u -> p a r u", a=2),
+        in_=bank[:].rearrange("p (a u) r -> p a r u", a=2),
+    )
+
+
+def tile_similargcn_pb_k_kernel(tc, weight, hid, W2, b2, out):
+    nc = tc.nc
+    with (
+        tc.tile_pool(name="const", bufs=1) as const,
+        tc.tile_pool(name="keep", bufs=1) as keep,
+        tc.tile_pool(name="raw", bufs=3) as raw,
+        tc.tile_pool(name="stage", bufs=2) as stage,
+        tc.psum_pool(name="sums", bufs=1) as sums,
+        tc.psum_pool(name="banks", bufs=4) as banks,
+    ):
+        identity = const.tile([P, P], F32)
+        make_identity(nc, identity[:])
+
+        weight_raw = const.tile([P, NODE_TILES, NODES], BF16)
+        nc.sync.dma_start(out=weight_raw[:], in_=weight.rearrange("(a p) j -> p a j", p=P))
+        weight_grouped = const.tile([P, NODES, 2], F32, align_bytes=64)
+        for pair in range(NODE_TILES // 2):
+            flip_two_row_tiles(
+                nc, banks, identity, weight_raw[:].bitcast(F32), 2 * pair, 0, weight_grouped
+            )
+        weight_codes = const.tile([P, NODES], U32, align_bytes=64)
+        weight_scales = const.tile([P, NODES], U8, align_bytes=64)
+        nc.vector.quantize_mx(
+            out=weight_codes[:].bitcast(FP8X4),
+            scales=weight_scales[:],
+            in_=weight_grouped[:].rearrange("p m u -> p (m u)").bitcast(BF16),
+        )
+
+        bias_rows = const.tile([P, P], BF16)
+        nc.vector.memset(bias_rows[:], 0.0)
+        nc.sync.dma_start(out=bias_rows[0:OUT_TILES, :], in_=b2.rearrange("(a p) -> a p", p=P))
+        bias_rows_f32 = const.tile([P, P], F32)
+        nc.vector.tensor_copy(out=bias_rows_f32[:], in_=bias_rows[:])
+        bias_bank = banks.tile([P, PACK, P], F32, tag="bank")
+        nc.tensor.transpose(bias_bank[:, 0, :], bias_rows_f32[:], identity[:])
+        bias = const.tile([P, OUT_TILES], F32)
+        nc.vector.tensor_copy(out=bias[:], in_=bias_bank[:, 0, 0:OUT_TILES])
+
+        agg_codes = keep.tile([P, PASSES, NODES], U32, align_bytes=64)
+        agg_scales = keep.tile([P, PASSES, NODES], U8, align_bytes=64)
+        result = keep.tile([P, OUT_TILES, PIXELS], F32)
+        out_rows = out.rearrange("x (a p) h w -> p (x a) (h w)", p=P)
+
+        for first_tile, n_tiles in ((0, FIRST_GROUP), (FIRST_GROUP, OUT_TILES - FIRST_GROUP)):
+            acc = [
+                sums.tile([P, NODES], F32, name="acc%d" % a, tag="acc%d" % a) for a in range(n_tiles)
+            ]
+            for c in range(CHUNKS):
+                cols = slice(c * CHUNK, (c + 1) * CHUNK)
+
+                if first_tile == 0:
+                    hid_raw = raw.tile([P, PACK, CHUNK], BF16)
+                    for u in range(2):
+                        nc.sync.dma_start(
+                            out=hid_raw[:, 2 * u : 2 * u + 2, :],
+                            in_=hid[u * HALF : (u + 1) * HALF, cols].rearrange("(q e) f -> q e f", e=2),
+                        )
+                w2_raw = raw.tile([P, n_tiles, CHUNK], BF16, tag="w2_raw")
+                nc.sync.dma_start(
+                    out=w2_raw[:],
+                    in_=W2[first_tile * P : (first_tile + n_tiles) * P, cols].rearrange(
+                        "(a p) f -> p a f", p=P
+                    ),
+                )
+
+                if first_tile == 0:
+                    hid_grouped = stage.tile([P, CHUNK, PACK], BF16, align_bytes=64)
+                    nc.vector.tensor_copy(
+                        out=hid_grouped[:].rearrange("p (s e i) t -> p s e i t", e=2, i=P),
+                        in_=hid_raw[:].rearrange("p t (s i e) -> p s e i t", e=2, i=P),
+                    )
+                    hid_codes = stage.tile([P, CHUNK], U32, align_bytes=64)
+                    hid_scales = stage.tile([P, CHUNK], U8, align_bytes=64)
+                    nc.vector.quantize_mx(
+                        out=hid_codes[:].bitcast(FP8X4),
+                        scales=hid_scales[:],
+                        in_=hid_grouped[:].rearrange("p f t -> p (f t)"),
+                    )
+
+                for local in range(CHUNK_PASSES):
+                    g = c * CHUNK_PASSES + local
+
+                    w2_grouped = stage.tile([P, n_tiles * P, 2], F32, tag="w2_grouped", align_bytes=64)
+                    for pair in range(n_tiles // 2):
+                        flip_two_row_tiles(
+                            nc, banks, identity, w2_raw[:].bitcast(F32), 2 * pair, local * HALF, w2_grouped
+                        )
+                    w2_codes = stage.tile([P, n_tiles * P], U32, tag="w2_codes", align_bytes=64)
+                    w2_scales = stage.tile([P, n_tiles * P], U8, tag="w2_scales", align_bytes=64)
+                    nc.vector.quantize_mx(
+                        out=w2_codes[:].bitcast(FP8X4),
+                        scales=w2_scales[:],
+                        in_=w2_grouped[:].rearrange("p o u -> p (o u)").bitcast(BF16),
+                    )
+
+                    if first_tile == 0:
+                        agg_grouped = stage.tile([P, NODES, PACK], BF16, align_bytes=64)
+                        for mt in range(NODE_TILES):
+                            m_cols = slice(mt * P, (mt + 1) * P)
+                            bank = banks.tile([P, PACK, P], F32, tag="bank")
+                            for t in range(PACK):
+                                f_cols = slice((local * PACK + t) * P, (local * PACK + t + 1) * P)
+                                nc.tensor.matmul_mx(
+                                    out=bank[:, t, :],
+                                    lhsT=hid_codes[:, f_cols].bitcast(FP8X4),
+                                    lhsT_scale=hid_scales[:, f_cols],
+                                    rhs=weight_codes[:, m_cols].bitcast(FP8X4),
+                                    rhs_scale=weight_scales[:, m_cols],
+                                    start=True,
+                                    stop=True,
+                                )
+                            nc.scalar.copy(
+                                out=agg_grouped[:, m_cols, :], in_=bank[:].rearrange("p t m -> p m t")
+                            )
+                        nc.vector.quantize_mx(
+                            out=agg_codes[:, g, :].bitcast(FP8X4),
+                            scales=agg_scales[:, g, :],
+                            in_=agg_grouped[:].rearrange("p m t -> p (m t)"),
+                        )
+
+                    for a in range(n_tiles):
+                        o_cols = slice(a * P, (a + 1) * P)
+                        nc.tensor.matmul_mx(
+                            out=acc[a][:],
+                            lhsT=w2_codes[:, o_cols].bitcast(FP8X4),
+                            lhsT_scale=w2_scales[:, o_cols],
+                            rhs=agg_codes[:, g, :].bitcast(FP8X4),
+                            rhs_scale=agg_scales[:, g, :],
+                            start=(g == 0),
+                            stop=(g == PASSES - 1),
+                        )
+
+            for a in range(n_tiles):
+                o_tile = first_tile + a
+                peak = stage.tile([P, PIXELS], F32)
+                nc.vector.tensor_reduce(
+                    out=peak[:],
+                    in_=acc[a][:].rearrange("p (n q) -> p q n", q=PIXELS),
+                    axis=mybir.AxisListType.X,
+                    op=ALU.max,
+                )
+                biased = stage.tile([P, PIXELS], F32)
+                nc.vector.tensor_scalar(
+                    out=biased[:], in0=peak[:], scalar1=bias[:, o_tile : o_tile + 1], scalar2=None, op0=ALU.add
+                )
+                nc.vector.scalar_tensor_tensor(
+                    out=result[:, o_tile, :],
+                    in0=biased[:],
+                    scalar=SLOPE,
+                    in1=biased[:],
+                    op0=ALU.mult,
+                    op1=ALU.max,
+                )
+            done = slice(first_tile, first_tile + n_tiles)
+            nc.sync.dma_start(out=out_rows[:, done, :], in_=result[:, done, :])

@@ -16,7 +16,6 @@ HALF = K_PASS // 2
 NODES = 512
 HIDDEN = 8192
 OUT = 768
-SAMPLES = 8
 PIXELS = 64
 SLOPE = 0.01
 
@@ -25,8 +24,10 @@ OUT_TILES = OUT // P
 PASSES = HIDDEN // K_PASS
 CHUNK_PASSES = 2
 CHUNK = CHUNK_PASSES * K_PASS
-CHUNKS = HIDDEN // CHUNK
-FIRST_GROUP = 4
+CHUNKS = PASSES // CHUNK_PASSES
+GROUPS = ((0, 4), (4, 2))
+STEP_PAIRS = 8
+LOADS_AHEAD = 3
 
 FLOPS = 2 * NODES * NODES * HIDDEN + 2 * NODES * HIDDEN * OUT
 
@@ -51,139 +52,139 @@ def tile_similargcn_pb_k_kernel(tc, weight, hid, W2, b2, out):
     with (
         tc.tile_pool(name="const", bufs=1) as const,
         tc.tile_pool(name="keep", bufs=1) as keep,
-        tc.tile_pool(name="raw", bufs=3) as raw,
+        tc.tile_pool(name="raw", bufs=4) as raw,
         tc.tile_pool(name="stage", bufs=2) as stage,
+        tc.tile_pool(name="codes", bufs=3) as codes,
         tc.psum_pool(name="sums", bufs=1) as sums,
         tc.psum_pool(name="banks", bufs=4) as banks,
+        tc.manual_schedule(),
     ):
-        identity = const.tile([P, P], F32)
-        make_identity(nc, identity[:])
+        steps = []
+        for first_tile, n_tiles in GROUPS:
+            step_passes = STEP_PAIRS // n_tiles
+            for first_pass in range(0, PASSES, step_passes):
+                steps.append((first_tile, n_tiles, first_pass, step_passes))
 
-        weight_raw = const.tile([P, NODE_TILES, NODES], BF16)
-        nc.sync.dma_start(out=weight_raw[:], in_=weight.rearrange("(a p) j -> p a j", p=P))
-        weight_grouped = const.tile([P, NODES, 2], F32, align_bytes=64)
-        for pair in range(NODE_TILES // 2):
-            flip_two_row_tiles(
-                nc, banks, identity, weight_raw[:].bitcast(F32), 2 * pair, 0, weight_grouped
-            )
-        weight_codes = const.tile([P, NODES], U32, align_bytes=64)
-        weight_scales = const.tile([P, NODES], U8, align_bytes=64)
-        nc.vector.quantize_mx(
-            out=weight_codes[:].bitcast(FP8X4),
-            scales=weight_scales[:],
-            in_=weight_grouped[:].rearrange("p m u -> p (m u)").bitcast(BF16),
-        )
-
-        bias_rows = const.tile([P, P], BF16)
-        nc.vector.memset(bias_rows[:], 0.0)
-        nc.sync.dma_start(out=bias_rows[0:OUT_TILES, :], in_=b2.rearrange("(a p) -> a p", p=P))
-        bias_rows_f32 = const.tile([P, P], F32)
-        nc.vector.tensor_copy(out=bias_rows_f32[:], in_=bias_rows[:])
-        bias_bank = banks.tile([P, PACK, P], F32, tag="bank")
-        nc.tensor.transpose(bias_bank[:, 0, :], bias_rows_f32[:], identity[:])
-        bias = const.tile([P, OUT_TILES], F32)
-        nc.vector.tensor_copy(out=bias[:], in_=bias_bank[:, 0, 0:OUT_TILES])
+        hid_raw_of = {}
+        hid_grouped_of = {}
+        hid_codes_of = {}
+        w2_raw_of = {}
+        w2_grouped_of = {}
+        w2_codes_of = {}
+        acc_of = {}
 
         agg_codes = keep.tile([P, PASSES, NODES], U32, align_bytes=64)
         agg_scales = keep.tile([P, PASSES, NODES], U8, align_bytes=64)
         result = keep.tile([P, OUT_TILES, PIXELS], F32)
         out_rows = out.rearrange("x (a p) h w -> p (x a) (h w)", p=P)
 
-        for first_tile, n_tiles in ((0, FIRST_GROUP), (FIRST_GROUP, OUT_TILES - FIRST_GROUP)):
-            acc = [
-                sums.tile([P, NODES], F32, name="acc%d" % a, tag="acc%d" % a) for a in range(n_tiles)
-            ]
-            for c in range(CHUNKS):
-                cols = slice(c * CHUNK, (c + 1) * CHUNK)
+        def load(s):
+            if s < CHUNKS:
+                hid_raw = raw.tile([P, PACK, CHUNK], BF16)
+                for u in range(2):
+                    nc.sync.dma_start(
+                        out=hid_raw[:, 2 * u : 2 * u + 2, :],
+                        in_=hid[u * HALF : (u + 1) * HALF, s * CHUNK : (s + 1) * CHUNK].rearrange(
+                            "(q e) f -> q e f", e=2
+                        ),
+                    )
+                hid_raw_of[s] = hid_raw
+            first_tile, n_tiles, first_pass, step_passes = steps[s]
+            w2_raw = raw.tile([P, n_tiles, step_passes * K_PASS], BF16, tag="w2_raw")
+            nc.sync.dma_start(
+                out=w2_raw[:],
+                in_=W2[
+                    first_tile * P : (first_tile + n_tiles) * P,
+                    first_pass * K_PASS : (first_pass + step_passes) * K_PASS,
+                ].rearrange("(a p) f -> p a f", p=P),
+            )
+            w2_raw_of[s] = w2_raw
 
-                if first_tile == 0:
-                    hid_raw = raw.tile([P, PACK, CHUNK], BF16)
-                    for u in range(2):
-                        nc.sync.dma_start(
-                            out=hid_raw[:, 2 * u : 2 * u + 2, :],
-                            in_=hid[u * HALF : (u + 1) * HALF, cols].rearrange("(q e) f -> q e f", e=2),
-                        )
-                w2_raw = raw.tile([P, n_tiles, CHUNK], BF16, tag="w2_raw")
-                nc.sync.dma_start(
-                    out=w2_raw[:],
-                    in_=W2[first_tile * P : (first_tile + n_tiles) * P, cols].rearrange(
-                        "(a p) f -> p a f", p=P
-                    ),
+        def flip_w2(s):
+            first_tile, n_tiles, first_pass, step_passes = steps[s]
+            w2_grouped = stage.tile([P, step_passes, n_tiles * P, 2], F32, tag="w2_grouped", align_bytes=64)
+            for local in range(step_passes):
+                for pair in range(n_tiles // 2):
+                    flip_two_row_tiles(
+                        nc, banks, identity, w2_raw_of[s][:].bitcast(F32), 2 * pair, local * HALF,
+                        w2_grouped[:, local],
+                    )
+            w2_grouped_of[s] = w2_grouped
+
+        def quantise_w2(s):
+            first_tile, n_tiles, first_pass, step_passes = steps[s]
+            w2_codes = codes.tile([P, step_passes, n_tiles * P], U32, tag="w2_codes", align_bytes=64)
+            w2_scales = codes.tile([P, step_passes, n_tiles * P], U8, tag="w2_scales", align_bytes=64)
+            nc.vector.quantize_mx(
+                out=w2_codes[:].rearrange("p l o -> p (l o)").bitcast(FP8X4),
+                scales=w2_scales[:].rearrange("p l o -> p (l o)"),
+                in_=w2_grouped_of[s][:].rearrange("p l o u -> p (l o u)").bitcast(BF16),
+            )
+            w2_codes_of[s] = (w2_codes, w2_scales)
+
+        def regroup_hid(c):
+            hid_grouped = stage.tile([P, CHUNK, PACK], BF16, align_bytes=64)
+            nc.vector.tensor_copy(
+                out=hid_grouped[:].rearrange("p (s e i) t -> p s e i t", e=2, i=P),
+                in_=hid_raw_of[c][:].rearrange("p t (s i e) -> p s e i t", e=2, i=P),
+            )
+            hid_grouped_of[c] = hid_grouped
+
+        def quantise_hid(c):
+            hid_codes = stage.tile([P, CHUNK], U32, align_bytes=64)
+            hid_scales = stage.tile([P, CHUNK], U8, align_bytes=64)
+            nc.vector.quantize_mx(
+                out=hid_codes[:].bitcast(FP8X4),
+                scales=hid_scales[:],
+                in_=hid_grouped_of[c][:].rearrange("p f t -> p (f t)"),
+            )
+            hid_codes_of[c] = (hid_codes, hid_scales)
+
+        def aggregate(c, local, mt, agg_grouped):
+            hid_codes, hid_scales = hid_codes_of[c]
+            m_cols = slice(mt * P, (mt + 1) * P)
+            bank = banks.tile([P, PACK, P], F32, tag="bank")
+            for t in range(PACK):
+                f_cols = slice((local * PACK + t) * P, (local * PACK + t + 1) * P)
+                nc.tensor.matmul_mx(
+                    out=bank[:, t, :],
+                    lhsT=hid_codes[:, f_cols].bitcast(FP8X4),
+                    lhsT_scale=hid_scales[:, f_cols],
+                    rhs=weight_codes[:, m_cols].bitcast(FP8X4),
+                    rhs_scale=weight_scales[:, m_cols],
+                    start=True,
+                    stop=True,
                 )
+            if local == CHUNK_PASSES - 1 and mt == NODE_TILES - 1:
+                nc.vector.tensor_copy(out=agg_grouped[:, m_cols, :], in_=bank[:].rearrange("p t m -> p m t"))
+            else:
+                nc.scalar.copy(out=agg_grouped[:, m_cols, :], in_=bank[:].rearrange("p t m -> p m t"))
 
-                if first_tile == 0:
-                    hid_grouped = stage.tile([P, CHUNK, PACK], BF16, align_bytes=64)
-                    nc.vector.tensor_copy(
-                        out=hid_grouped[:].rearrange("p (s e i) t -> p s e i t", e=2, i=P),
-                        in_=hid_raw[:].rearrange("p t (s i e) -> p s e i t", e=2, i=P),
-                    )
-                    hid_codes = stage.tile([P, CHUNK], U32, align_bytes=64)
-                    hid_scales = stage.tile([P, CHUNK], U8, align_bytes=64)
-                    nc.vector.quantize_mx(
-                        out=hid_codes[:].bitcast(FP8X4),
-                        scales=hid_scales[:],
-                        in_=hid_grouped[:].rearrange("p f t -> p (f t)"),
-                    )
+        def multiply(s, i):
+            first_tile, n_tiles, first_pass, step_passes = steps[s]
+            local = i // n_tiles
+            a = i % n_tiles
+            g = first_pass + local
+            if g == 0:
+                acc_of[first_tile + a] = sums.tile([P, NODES], F32, name="acc%d" % a, tag="acc%d" % a)
+            w2_codes, w2_scales = w2_codes_of[s]
+            o_cols = slice(a * P, (a + 1) * P)
+            nc.tensor.matmul_mx(
+                out=acc_of[first_tile + a][:],
+                lhsT=w2_codes[:, local, o_cols].bitcast(FP8X4),
+                lhsT_scale=w2_scales[:, local, o_cols],
+                rhs=agg_codes[:, g, :].bitcast(FP8X4),
+                rhs_scale=agg_scales[:, g, :],
+                start=(g == 0),
+                stop=(g == PASSES - 1),
+            )
 
-                for local in range(CHUNK_PASSES):
-                    g = c * CHUNK_PASSES + local
-
-                    w2_grouped = stage.tile([P, n_tiles * P, 2], F32, tag="w2_grouped", align_bytes=64)
-                    for pair in range(n_tiles // 2):
-                        flip_two_row_tiles(
-                            nc, banks, identity, w2_raw[:].bitcast(F32), 2 * pair, local * HALF, w2_grouped
-                        )
-                    w2_codes = stage.tile([P, n_tiles * P], U32, tag="w2_codes", align_bytes=64)
-                    w2_scales = stage.tile([P, n_tiles * P], U8, tag="w2_scales", align_bytes=64)
-                    nc.vector.quantize_mx(
-                        out=w2_codes[:].bitcast(FP8X4),
-                        scales=w2_scales[:],
-                        in_=w2_grouped[:].rearrange("p o u -> p (o u)").bitcast(BF16),
-                    )
-
-                    if first_tile == 0:
-                        agg_grouped = stage.tile([P, NODES, PACK], BF16, align_bytes=64)
-                        for mt in range(NODE_TILES):
-                            m_cols = slice(mt * P, (mt + 1) * P)
-                            bank = banks.tile([P, PACK, P], F32, tag="bank")
-                            for t in range(PACK):
-                                f_cols = slice((local * PACK + t) * P, (local * PACK + t + 1) * P)
-                                nc.tensor.matmul_mx(
-                                    out=bank[:, t, :],
-                                    lhsT=hid_codes[:, f_cols].bitcast(FP8X4),
-                                    lhsT_scale=hid_scales[:, f_cols],
-                                    rhs=weight_codes[:, m_cols].bitcast(FP8X4),
-                                    rhs_scale=weight_scales[:, m_cols],
-                                    start=True,
-                                    stop=True,
-                                )
-                            nc.scalar.copy(
-                                out=agg_grouped[:, m_cols, :], in_=bank[:].rearrange("p t m -> p m t")
-                            )
-                        nc.vector.quantize_mx(
-                            out=agg_codes[:, g, :].bitcast(FP8X4),
-                            scales=agg_scales[:, g, :],
-                            in_=agg_grouped[:].rearrange("p m t -> p (m t)"),
-                        )
-
-                    for a in range(n_tiles):
-                        o_cols = slice(a * P, (a + 1) * P)
-                        nc.tensor.matmul_mx(
-                            out=acc[a][:],
-                            lhsT=w2_codes[:, o_cols].bitcast(FP8X4),
-                            lhsT_scale=w2_scales[:, o_cols],
-                            rhs=agg_codes[:, g, :].bitcast(FP8X4),
-                            rhs_scale=agg_scales[:, g, :],
-                            start=(g == 0),
-                            stop=(g == PASSES - 1),
-                        )
-
-            for a in range(n_tiles):
-                o_tile = first_tile + a
+        def finish(first_tile, n_tiles):
+            for o_tile in range(first_tile, first_tile + n_tiles):
                 peak = stage.tile([P, PIXELS], F32)
                 nc.vector.tensor_reduce(
                     out=peak[:],
-                    in_=acc[a][:].rearrange("p (n q) -> p q n", q=PIXELS),
+                    in_=acc_of[o_tile][:].rearrange("p (n q) -> p q n", q=PIXELS),
                     axis=mybir.AxisListType.X,
                     op=ALU.max,
                 )
@@ -201,3 +202,66 @@ def tile_similargcn_pb_k_kernel(tc, weight, hid, W2, b2, out):
                 )
             done = slice(first_tile, first_tile + n_tiles)
             nc.sync.dma_start(out=out_rows[:, done, :], in_=result[:, done, :])
+
+        identity = const.tile([P, P], F32)
+        make_identity(nc, identity[:])
+        bias_rows = const.tile([P, P], BF16)
+        nc.vector.memset(bias_rows[:], 0.0)
+        nc.sync.dma_start(out=bias_rows[0:OUT_TILES, :], in_=b2.rearrange("(a p) -> a p", p=P))
+        weight_raw = const.tile([P, NODE_TILES, NODES], BF16)
+        nc.sync.dma_start(out=weight_raw[:], in_=weight.rearrange("(a p) j -> p a j", p=P))
+        for s in range(LOADS_AHEAD):
+            load(s)
+
+        bias_rows_f32 = const.tile([P, P], F32)
+        nc.vector.tensor_copy(out=bias_rows_f32[:], in_=bias_rows[:])
+        bias_bank = banks.tile([P, PACK, P], F32, tag="bank")
+        nc.tensor.transpose(bias_bank[:, 0, :], bias_rows_f32[:], identity[:])
+        bias = const.tile([P, OUT_TILES], F32)
+        nc.vector.tensor_copy(out=bias[:], in_=bias_bank[:, 0, 0:OUT_TILES])
+
+        weight_grouped = const.tile([P, NODES, 2], F32, align_bytes=64)
+        for pair in range(NODE_TILES // 2):
+            flip_two_row_tiles(nc, banks, identity, weight_raw[:].bitcast(F32), 2 * pair, 0, weight_grouped)
+        weight_codes = const.tile([P, NODES], U32, align_bytes=64)
+        weight_scales = const.tile([P, NODES], U8, align_bytes=64)
+        nc.vector.quantize_mx(
+            out=weight_codes[:].bitcast(FP8X4),
+            scales=weight_scales[:],
+            in_=weight_grouped[:].rearrange("p m u -> p (m u)").bitcast(BF16),
+        )
+        flip_w2(0)
+        regroup_hid(0)
+        quantise_w2(0)
+        quantise_hid(0)
+
+        for s in range(len(steps) + 1):
+            if s + LOADS_AHEAD < len(steps):
+                load(s + LOADS_AHEAD)
+            if s + 1 < len(steps):
+                flip_w2(s + 1)
+                if s + 1 < CHUNKS:
+                    regroup_hid(s + 1)
+                quantise_w2(s + 1)
+                if s + 1 < CHUNKS:
+                    quantise_hid(s + 1)
+            for i in range(STEP_PAIRS):
+                if s < CHUNKS:
+                    local = i // NODE_TILES
+                    mt = i % NODE_TILES
+                    if mt == 0:
+                        agg_grouped = stage.tile([P, NODES, PACK], BF16, align_bytes=64)
+                    aggregate(s, local, mt, agg_grouped)
+                    if mt == NODE_TILES - 1:
+                        g = s * CHUNK_PASSES + local
+                        nc.vector.quantize_mx(
+                            out=agg_codes[:, g, :].bitcast(FP8X4),
+                            scales=agg_scales[:, g, :],
+                            in_=agg_grouped[:].rearrange("p m t -> p (m t)"),
+                        )
+                if s >= 1:
+                    multiply(s - 1, i)
+            if s >= 1:
+                first_tile, n_tiles, first_pass, step_passes = steps[s - 1]
+                if first_pass + step_passes == PASSES:
+                    finish(first_tile, n_tiles)

@@ -125,8 +125,8 @@ def tile_similargcn_pb_k_kernel(tc, weight, hid, W2, b2, out):
         def regroup_hid(c):
             hid_grouped = stage.tile([P, CHUNK, PACK], BF16, align_bytes=64)
             nc.vector.tensor_copy(
-                out=hid_grouped[:].rearrange("p (s e i) t -> p s e i t", e=2, i=P),
-                in_=hid_raw_of[c][:].rearrange("p t (s i e) -> p s e i t", e=2, i=P),
+                out=hid_grouped[:].rearrange("p (e c i) t -> p c t i e", e=2, i=2),
+                in_=hid_raw_of[c][:].rearrange("p t (c i e) -> p c t i e", e=2, i=2),
             )
             hid_grouped_of[c] = hid_grouped
 
@@ -145,7 +145,10 @@ def tile_similargcn_pb_k_kernel(tc, weight, hid, W2, b2, out):
             m_cols = slice(mt * P, (mt + 1) * P)
             bank = banks.tile([P, PACK, P], F32, tag="bank")
             for t in range(PACK):
-                f_cols = slice((local * PACK + t) * P, (local * PACK + t + 1) * P)
+                u = t // 2
+                e = t % 2
+                first = e * (CHUNK // 2) + (2 * local + u) * P
+                f_cols = slice(first, first + P)
                 nc.tensor.matmul_mx(
                     out=bank[:, t, :],
                     lhsT=hid_codes[:, f_cols].bitcast(FP8X4),

@@ -228,32 +228,30 @@ def tile_similargcn_pb_k_kernel(tc, weight, hid, W2, b2, out):
             flip_two_row_tiles(nc, banks, identity, weight_raw[:].bitcast(F32), 2 * pair, 0, weight_grouped)
         weight_codes = const.tile([P, NODES], U32, align_bytes=64)
         weight_scales = const.tile([P, NODES], U8, align_bytes=64)
+        flip_w2(0)
+        regroup_hid(0)
         nc.vector.quantize_mx(
             out=weight_codes[:].bitcast(FP8X4),
             scales=weight_scales[:],
             in_=weight_grouped[:].rearrange("p m u -> p (m u)").bitcast(BF16),
         )
-        flip_w2(0)
-        regroup_hid(0)
-        quantise_w2(0)
         quantise_hid(0)
 
         for s in range(len(steps) + 1):
             if s + LOADS_AHEAD < len(steps):
                 load(s + LOADS_AHEAD)
-            if s + 1 < len(steps):
-                flip_w2(s + 1)
-                if s + 1 < CHUNKS:
-                    regroup_hid(s + 1)
-                quantise_w2(s + 1)
-                if s + 1 < CHUNKS:
-                    quantise_hid(s + 1)
+            if s + 1 < CHUNKS:
+                regroup_hid(s + 1)
+            if s < len(steps):
+                quantise_w2(s)
+            if s + 1 < CHUNKS:
+                quantise_hid(s + 1)
             for i in range(STEP_PAIRS):
                 if s < CHUNKS:
                     local = i // NODE_TILES
                     mt = i % NODE_TILES
                     if mt == 0:
-                        agg_grouped = stage.tile([P, NODES, PACK], BF16, align_bytes=64)
+                        agg_grouped = stage.tile([P, NODES, PACK], BF16, bufs=3, align_bytes=64)
                     aggregate(s, local, mt, agg_grouped)
                     if mt == NODE_TILES - 1:
                         g = s * CHUNK_PASSES + local
@@ -264,6 +262,8 @@ def tile_similargcn_pb_k_kernel(tc, weight, hid, W2, b2, out):
                         )
                 if s >= 1:
                     multiply(s - 1, i)
+            if s + 1 < len(steps):
+                flip_w2(s + 1)
             if s >= 1:
                 first_tile, n_tiles, first_pass, step_passes = steps[s - 1]
                 if first_pass + step_passes == PASSES:

@@ -158,10 +158,7 @@ def tile_similargcn_pb_k_kernel(tc, weight, hid, W2, b2, out):
                     start=True,
                     stop=True,
                 )
-            if local == CHUNK_PASSES - 1 and mt == NODE_TILES - 1:
-                nc.vector.tensor_copy(out=agg_grouped[:, m_cols, :], in_=bank[:].rearrange("p t m -> p m t"))
-            else:
-                nc.scalar.copy(out=agg_grouped[:, m_cols, :], in_=bank[:].rearrange("p t m -> p m t"))
+            nc.scalar.copy(out=agg_grouped[:, m_cols, :], in_=bank[:].rearrange("p t m -> p m t"))
 
         def multiply(s, i):
             first_tile, n_tiles, first_pass, step_passes = steps[s]

import concourse.mybir as mybir
from concourse.masks import make_identity

F32 = mybir.dt.float32
BF16 = mybir.dt.bfloat16
U32 = mybir.dt.uint32
U8 = mybir.dt.uint8
FP8X4 = mybir.dt.float8_e4m3fn_x4
ALU = mybir.AluOpType

P = 128
PACK = 4
K_PASS = P * PACK
HALF = K_PASS // 2

NODES = 512
HIDDEN = 8192
OUT = 768
PIXELS = 64
SLOPE = 0.01

NODE_TILES = NODES // P
OUT_TILES = OUT // P
PASSES = HIDDEN // K_PASS
CHUNK_PASSES = 2
CHUNK = CHUNK_PASSES * K_PASS
CHUNKS = PASSES // CHUNK_PASSES
GROUPS = ((0, 4), (4, 2))
STEP_PAIRS = 8
LOADS_AHEAD = 3

FLOPS = 2 * NODES * NODES * HIDDEN + 2 * NODES * HIDDEN * OUT


def flip_two_row_tiles(nc, banks, identity, words, tile0, word0, grouped_words):
    bank = banks.tile([P, PACK, P], F32, tag="bank")
    for a in range(2):
        for u in range(2):
            nc.tensor.transpose(
                bank[:, 2 * a + u, :],
                words[:, tile0 + a, word0 + u * P : word0 + (u + 1) * P],
                identity[:],
            )
    nc.scalar.copy(
        out=grouped_words[:, tile0 * P : (tile0 + 2) * P, :].rearrange("p (a r) u -> p a r u", a=2),
        in_=bank[:].rearrange("p (a u) r -> p a r u", a=2),
    )


def tile_similargcn_pb_k_kernel(tc, weight, hid, W2, b2, out):
    nc = tc.nc
    with (
        tc.tile_pool(name="const", bufs=1) as const,
        tc.tile_pool(name="keep", bufs=1) as keep,
        tc.tile_pool(name="raw", bufs=4) as raw,
        tc.tile_pool(name="stage", bufs=2) as stage,
        tc.tile_pool(name="codes", bufs=3) as codes,
        tc.psum_pool(name="sums", bufs=1) as sums,
        tc.psum_pool(name="banks", bufs=4) as banks,
        tc.manual_schedule(),
    ):
        steps = []
        for first_tile, n_tiles in GROUPS:
            step_passes = STEP_PAIRS // n_tiles
            for first_pass in range(0, PASSES, step_passes):
                steps.append((first_tile, n_tiles, first_pass, step_passes))

        hid_raw_of = {}
        hid_grouped_of = {}
        hid_codes_of = {}
        w2_raw_of = {}
        w2_grouped_of = {}
        w2_codes_of = {}
        acc_of = {}

        agg_codes = keep.tile([P, PASSES, NODES], U32, align_bytes=64)
        agg_scales = keep.tile([P, PASSES, NODES], U8, align_bytes=64)
        result = keep.tile([P, OUT_TILES, PIXELS], F32)
        out_rows = out.rearrange("x (a p) h w -> p (x a) (h w)", p=P)

        def load(s):
            if s < CHUNKS:
                hid_raw = raw.tile([P, PACK, CHUNK], BF16)
                for u in range(2):
                    nc.sync.dma_start(
                        out=hid_raw[:, 2 * u : 2 * u + 2, :],
                        in_=hid[u * HALF : (u + 1) * HALF, s * CHUNK : (s + 1) * CHUNK].rearrange(
                            "(q e) f -> q e f", e=2
                        ),
                    )
                hid_raw_of[s] = hid_raw
            first_tile, n_tiles, first_pass, step_passes = steps[s]
            w2_raw = raw.tile([P, n_tiles, step_passes * K_PASS], BF16, tag="w2_raw")
            nc.sync.dma_start(
                out=w2_raw[:],
                in_=W2[
                    first_tile * P : (first_tile + n_tiles) * P,
                    first_pass * K_PASS : (first_pass + step_passes) * K_PASS,
                ].rearrange("(a p) f -> p a f", p=P),
            )
            w2_raw_of[s] = w2_raw

        def flip_w2(s):
            first_tile, n_tiles, first_pass, step_passes = steps[s]
            w2_grouped = stage.tile([P, step_passes, n_tiles * P, 2], F32, tag="w2_grouped", align_bytes=64)
            for local in range(step_passes):
                for pair in range(n_tiles // 2):
                    flip_two_row_tiles(
                        nc, banks, identity, w2_raw_of[s][:].bitcast(F32), 2 * pair, local * HALF,
                        w2_grouped[:, local],
                    )
            w2_grouped_of[s] = w2_grouped

        def quantise_w2(s):
            first_tile, n_tiles, first_pass, step_passes = steps[s]
            w2_codes = codes.tile([P, step_passes, n_tiles * P], U32, tag="w2_codes", align_bytes=64)
            w2_scales = codes.tile([P, step_passes, n_tiles * P], U8, tag="w2_scales", align_bytes=64)
            nc.vector.quantize_mx(
                out=w2_codes[:].rearrange("p l o -> p (l o)").bitcast(FP8X4),
                scales=w2_scales[:].rearrange("p l o -> p (l o)"),
                in_=w2_grouped_of[s][:].rearrange("p l o u -> p (l o u)").bitcast(BF16),
            )
            w2_codes_of[s] = (w2_codes, w2_scales)

        def regroup_hid(c):
            hid_grouped = stage.tile([P, CHUNK, PACK], BF16, align_bytes=64)
            nc.vector.tensor_copy(
                out=hid_grouped[:].rearrange("p (e c i) t -> p c t i e", e=2, i=2),
                in_=hid_raw_of[c][:].rearrange("p t (c i e) -> p c t i e", e=2, i=2),
            )
            hid_grouped_of[c] = hid_grouped

        def quantise_hid(c):
            hid_codes = stage.tile([P, CHUNK], U32, align_bytes=64)
            hid_scales = stage.tile([P, CHUNK], U8, align_bytes=64)
            nc.vector.quantize_mx(
                out=hid_codes[:].bitcast(FP8X4),
                scales=hid_scales[:],
                in_=hid_grouped_of[c][:].rearrange("p f t -> p (f t)"),
            )
            hid_codes_of[c] = (hid_codes, hid_scales)

        def aggregate(c, local, mt, agg_grouped):
            hid_codes, hid_scales = hid_codes_of[c]
            m_cols = slice(mt * P, (mt + 1) * P)
            bank = banks.tile([P, PACK, P], F32, tag="bank")
            for t in range(PACK):
                u = t // 2
                e = t % 2
                first = e * (CHUNK // 2) + (2 * local + u) * P
                f_cols = slice(first, first + P)
                nc.tensor.matmul_mx(
                    out=bank[:, t, :],
                    lhsT=hid_codes[:, f_cols].bitcast(FP8X4),
                    lhsT_scale=hid_scales[:, f_cols],
                    rhs=weight_codes[:, m_cols].bitcast(FP8X4),
                    rhs_scale=weight_scales[:, m_cols],
                    start=True,
                    stop=True,
                )
            nc.scalar.copy(out=agg_grouped[:, m_cols, :], in_=bank[:].rearrange("p t m -> p m t"))

        def multiply(s, i):
            first_tile, n_tiles, first_pass, step_passes = steps[s]
            local = i // n_tiles
            a = i % n_tiles
            g = first_pass + local
            if g == 0:
                acc_of[first_tile + a] = sums.tile([P, NODES], F32, name="acc%d" % a, tag="acc%d" % a)
            w2_codes, w2_scales = w2_codes_of[s]
            o_cols = slice(a * P, (a + 1) * P)
            nc.tensor.matmul_mx(
                out=acc_of[first_tile + a][:],
                lhsT=w2_codes[:, local, o_cols].bitcast(FP8X4),
                lhsT_scale=w2_scales[:, local, o_cols],
                rhs=agg_codes[:, g, :].bitcast(FP8X4),
                rhs_scale=agg_scales[:, g, :],
                start=(g == 0),
                stop=(g == PASSES - 1),
            )

        def finish(first_tile, n_tiles):
            for o_tile in range(first_tile, first_tile + n_tiles):
                peak = stage.tile([P, PIXELS], F32)
                nc.vector.tensor_reduce(
                    out=peak[:],
                    in_=acc_of[o_tile][:].rearrange("p (n q) -> p q n", q=PIXELS),
                    axis=mybir.AxisListType.X,
                    op=ALU.max,
                )
                biased = stage.tile([P, PIXELS], F32)
                nc.vector.tensor_scalar(
                    out=biased[:], in0=peak[:], scalar1=bias[:, o_tile : o_tile + 1], scalar2=None, op0=ALU.add
                )
                nc.vector.scalar_tensor_tensor(
                    out=result[:, o_tile, :],
                    in0=biased[:],
                    scalar=SLOPE,
                    in1=biased[:],
                    op0=ALU.mult,
                    op1=ALU.max,
                )
            done = slice(first_tile, first_tile + n_tiles)
            nc.sync.dma_start(out=out_rows[:, done, :], in_=result[:, done, :])

        identity = const.tile([P, P], F32)
        make_identity(nc, identity[:])
        bias_rows = const.tile([P, P], BF16)
        nc.vector.memset(bias_rows[:], 0.0)
        nc.sync.dma_start(out=bias_rows[0:OUT_TILES, :], in_=b2.rearrange("(a p) -> a p", p=P))
        weight_raw = const.tile([P, NODE_TILES, NODES], BF16)
        nc.sync.dma_start(out=weight_raw[:], in_=weight.rearrange("(a p) j -> p a j", p=P))
        for s in range(LOADS_AHEAD):
            load(s)

        bias_rows_f32 = const.tile([P, P], F32)
        nc.vector.tensor_copy(out=bias_rows_f32[:], in_=bias_rows[:])
        bias_bank = banks.tile([P, PACK, P], F32, tag="bank")
        nc.tensor.transpose(bias_bank[:, 0, :], bias_rows_f32[:], identity[:])
        bias = const.tile([P, OUT_TILES], F32)
        nc.vector.tensor_copy(out=bias[:], in_=bias_bank[:, 0, 0:OUT_TILES])

        weight_grouped = const.tile([P, NODES, 2], F32, align_bytes=64)
        for pair in range(NODE_TILES // 2):
            flip_two_row_tiles(nc, banks, identity, weight_raw[:].bitcast(F32), 2 * pair, 0, weight_grouped)
        weight_codes = const.tile([P, NODES], U32, align_bytes=64)
        weight_scales = const.tile([P, NODES], U8, align_bytes=64)
        flip_w2(0)
        regroup_hid(0)
        nc.vector.quantize_mx(
            out=weight_codes[:].bitcast(FP8X4),
            scales=weight_scales[:],
            in_=weight_grouped[:].rearrange("p m u -> p (m u)").bitcast(BF16),
        )
        quantise_hid(0)

        for s in range(len(steps) + 1):
            if s + LOADS_AHEAD < len(steps):
                load(s + LOADS_AHEAD)
            if s + 1 < CHUNKS:
                regroup_hid(s + 1)
            if s < len(steps):
                quantise_w2(s)
            if s + 1 < CHUNKS:
                quantise_hid(s + 1)
            for i in range(STEP_PAIRS):
                if s < CHUNKS:
                    local = i // NODE_TILES
                    mt = i % NODE_TILES
                    if mt == 0:
                        agg_grouped = stage.tile([P, NODES, PACK], BF16, bufs=3, align_bytes=64)
                    aggregate(s, local, mt, agg_grouped)
                    if mt == NODE_TILES - 1:
                        g = s * CHUNK_PASSES + local
                        nc.vector.quantize_mx(
                            out=agg_codes[:, g, :].bitcast(FP8X4),
                            scales=agg_scales[:, g, :],
                            in_=agg_grouped[:].rearrange("p m t -> p (m t)"),
                        )
                if s >= 1:
                    multiply(s - 1, i)
            if s + 1 < len(steps):
                flip_w2(s + 1)
            if s >= 1:
                first_tile, n_tiles, first_pass, step_passes = steps[s - 1]
                if first_pass + step_passes == PASSES:
                    finish(first_tile, n_tiles)
